import numpy as np
import ml_dtypes


def mxq(x, axis, fmt="e4m3"):
    dtype, down = {"e4m3": (ml_dtypes.float8_e4m3fn, 7), "e5m2": (ml_dtypes.float8_e5m2, 14)}[fmt]
    v = np.moveaxis(np.asarray(x, np.float32).astype(ml_dtypes.bfloat16).astype(np.float64), axis, -1)
    blocks = v.reshape(v.shape[:-1] + (-1, 32))
    amax = np.abs(blocks).max(-1, keepdims=True)
    byte = np.maximum(np.where(amax > 0, np.frexp(amax)[1] - 1 + 127, 0) - down, 1)
    scale = np.exp2(byte - 127.0)
    codes = (blocks / scale).astype(np.float32).astype(dtype).astype(np.float64)
    return np.moveaxis((codes * scale).reshape(v.shape), -1, axis)


WIDE = False


def mx_kscale(k):
    if not WIDE:
        return np.ones(k)
    levels = np.array([10, -10, 5, -5, 0])
    a = np.random.permutation(np.resize(levels, k // 512 * 4)).reshape(k // 512, 4)
    idx = np.arange(k)
    return np.exp2(a[idx // 512, idx % 128 // 32])


BF16 = ml_dtypes.bfloat16


def bf(x):
    return np.asarray(x, np.float32).astype(BF16)


def f64(x):
    return np.asarray(x).astype(np.float64)


E2M1 = np.array([0.0, 0.5, 1.0, 1.5, 2.0, 3.0, 4.0, 6.0, -0.0, -0.5, -1.0, -1.5, -2.0, -3.0, -4.0, -6.0])


def pack_weight(w, fmt):
    k, n = w.shape
    w = f64(bf(w)).reshape(k // 32, 32, n)
    amax = np.abs(w).max(1)
    if fmt == "e4m3":
        byte = np.frexp(amax)[1] - 1 + 127 - 7
    else:
        mant, ex = np.frexp(amax / 6.0)
        byte = np.where(mant > 0.5, ex, ex - 1) + 127
    byte = np.clip(np.where(amax > 0, byte, 1), 1, 254)
    scaled = (w * np.exp2(127.0 - byte)[:, None, :]).reshape(k, n).astype(np.float32)
    by_word = np.ascontiguousarray(scaled.reshape(k // 512, 128, 4, n).transpose(0, 1, 3, 2))
    if fmt == "e4m3":
        words = by_word.astype(ml_dtypes.float8_e4m3fn).view(np.uint8)
    else:
        c = by_word.astype(ml_dtypes.float4_e2m1fn).view(np.uint8) & 0xF
        words = c[..., 0::2] | (c[..., 1::2] << 4)
    return np.ascontiguousarray(words), np.ascontiguousarray(byte.astype(np.uint8).reshape(k // 512, 16, n))


def unpack_weight(words, scales, fmt):
    g, p, n, _ = words.shape
    if fmt == "e4m3":
        vals = np.ascontiguousarray(words).view(ml_dtypes.float8_e4m3fn).astype(np.float64)
    else:
        nib = np.empty((g, p, n, 4), np.uint8)
        nib[..., 0::2] = words & 0xF
        nib[..., 1::2] = words >> 4
        vals = E2M1[nib]
    vals = vals * np.repeat(np.exp2(scales.astype(np.float64) - 127.0), 8, axis=1)[..., None]
    return vals.transpose(0, 1, 3, 2).reshape(g * 512, n)


B, N, D, H, DH, WS = 1, 1024, 1024, 8, 128, 512
INNER = H * DH
NW = N // WS
BW = B * NW
FMT = "e4m3"


def elu(u):
    return np.where(u > 0.0, u, np.exp(np.minimum(u, 0.0)) - 1.0)


def heads(t):
    return t.reshape(BW, WS, H, DH).transpose(0, 2, 1, 3)


def setup_inputs():
    s = mx_kscale(D)
    x = bf(np.random.standard_normal((B, N, D)) * s)
    k_words, k_scales = pack_weight(np.random.standard_normal((D, INNER)) / np.sqrt(D) / s[:, None], FMT)
    v_words, v_scales = pack_weight(np.random.standard_normal((D, INNER)) * 0.3 / np.sqrt(D * WS) / s[:, None], FMT)
    return {"x": x,
            "w_k_words": k_words, "w_k_scales": k_scales,
            "w_v_words": v_words, "w_v_scales": v_scales}


def reference(x, w_k_words, w_k_scales, w_v_words, w_v_scales):
    xq = mxq(f64(x).reshape(BW, WS, D), 2, "e4m3")
    k = heads(xq @ unpack_weight(w_k_words, w_k_scales, FMT))
    v = heads(xq @ unpack_weight(w_v_words, w_v_scales, FMT))
    kf = elu(k) + 1.0
    return mxq(kf, 2, "e4m3").transpose(0, 1, 3, 2) @ mxq(v, 2, "e4m3")

@@ -1,0 +1,212 @@
+from contextlib import ExitStack
+
+import concourse.masks as masks
+import concourse.mybir as mybir
+
+F32 = mybir.dt.float32
+BF16 = mybir.dt.bfloat16
+I32 = mybir.dt.int32
+U32 = mybir.dt.uint32
+U8 = mybir.dt.uint8
+FP8X4 = mybir.dt.float8_e4m3fn_x4
+ACT = mybir.ActivationFunctionType
+ALU = mybir.AluOpType
+
+P = 128
+PACK = 4
+WINDOWS = 2
+TOKEN_TILES = PACK
+FEATURES = 1024
+PASSES = FEATURES // (P * PACK)
+HALF_WORDS = 2
+HEADS = 8
+HEAD_DIM = 128
+INNER = HEADS * HEAD_DIM
+KEYS, VALUES = 0, 1
+GROUP = 4
+CONTEXT_LAG = 2
+X_AHEAD = (3, 5)
+
+FLOPS = 2 * 2 * WINDOWS * 512 * FEATURES * INNER + 2 * WINDOWS * HEADS * 512 * HEAD_DIM * HEAD_DIM
+
+
+def tile_localcontextprocessor_pa_kernel(
+    tc, x, w_k_words, w_k_scales, w_v_words, w_v_scales, out
+):
+    nc = tc.nc
+    with ExitStack() as stack:
+        stack.enter_context(tc.manual_schedule())
+        keep = stack.enter_context(tc.tile_pool(name="keep", bufs=1))
+        x_stage = stack.enter_context(tc.tile_pool(name="x_stage", bufs=4))
+        stage = stack.enter_context(tc.tile_pool(name="stage", bufs=3))
+        head_codes_pool = stack.enter_context(tc.tile_pool(name="head_codes", bufs=8))
+        store_pool = stack.enter_context(tc.tile_pool(name="store", bufs=2))
+        psum = stack.enter_context(tc.psum_pool(name="psum", bufs=8))
+
+        w_planes = keep.tile([P, INNER], U8, align_bytes=64)
+        nc.vector.memset(w_planes[:].bitcast(I32), 0)
+        zero = keep.tile([P, 1], F32)
+        one = keep.tile([P, 1], F32)
+        nc.vector.memset(zero[:], 0.0)
+        nc.scalar.activation(out=one[:], in_=zero[:], func=ACT.Exp)
+        identity = keep.tile([P, P], F32)
+        masks.make_identity(nc, identity[:])
+
+        x_rows = x[0].rearrange("(w p t) d -> w p t d", w=WINDOWS, t=TOKEN_TILES)
+        x_sb = {}
+
+        def load_x(w):
+            for half in range(2):
+                x_pair = keep.tile([P, 2, FEATURES], BF16, name="x_pair_%d_%d" % (w, half))
+                nc.sync.dma_start(out=x_pair[:], in_=x_rows[w][:, 2 * half : 2 * half + 2, :])
+                x_sb[(w, half)] = x_pair
+
+        w_codes = {
+            KEYS: keep.tile([P, PASSES, INNER], U32, name="w_k_codes", align_bytes=64),
+            VALUES: keep.tile([P, PASSES, INNER], U32, name="w_v_codes", align_bytes=64),
+        }
+        w_words = {KEYS: w_k_words, VALUES: w_v_words}
+        w_scales = {KEYS: w_k_scales, VALUES: w_v_scales}
+
+        def load_scales(kind):
+            for quadrant in range(4):
+                first = 32 * quadrant + 4 * PASSES * kind
+                nc.sync.dma_start(
+                    out=w_planes[first : first + 4 * PASSES, :].bitcast(I32),
+                    in_=w_scales[kind][:, 4 * quadrant : 4 * quadrant + 4, :].bitcast(I32),
+                )
+
+        def load_codes(kind, group):
+            first = group * GROUP * HEAD_DIM
+            last = first + GROUP * HEAD_DIM
+            code_bytes = w_words[kind].rearrange("g p n t -> p g (n t)")
+            nc.sync.dma_start(
+                out=w_codes[kind][:, :, first:last].bitcast(I32),
+                in_=code_bytes[:, :, PACK * first : PACK * last].bitcast(I32),
+            )
+
+        load_x(0)
+        load_scales(KEYS)
+        load_codes(KEYS, 0)
+        load_codes(VALUES, 0)
+        load_scales(VALUES)
+        load_x(1)
+        load_codes(KEYS, 1)
+        load_codes(VALUES, 1)
+
+        x_codes = {}
+
+        def quantise(grouped, codes, scales):
+            nc.vector.quantize_mx(out=codes.bitcast(FP8X4), scales=scales, in_=grouped)
+
+        def transpose_x(w, t):
+            words = x_sb[(w, t // 2)][:, t % 2, :].bitcast(F32)
+            flipped = psum.tile([P, PASSES, HALF_WORDS, P], F32, tag="bank")
+            for g in range(PASSES):
+                for u in range(HALF_WORDS):
+                    nc.tensor.transpose(
+                        flipped[:, g, u, :],
+                        words[:, 256 * g + u : 256 * (g + 1) : HALF_WORDS],
+                        identity[:],
+                    )
+            grouped = x_stage.tile([P, PASSES * P * PACK], BF16, align_bytes=64, tag="x_grouped")
+            copy = nc.vector.tensor_copy if t % 2 == 0 else nc.scalar.copy
+            copy(
+                out=grouped[:].bitcast(F32).rearrange(
+                    "p (g r u) -> p g r u", g=PASSES, u=HALF_WORDS
+                ),
+                in_=flipped[:].rearrange("p g u r -> p g r u"),
+            )
+            codes = keep.tile([P, PASSES * P], U32, name="x_codes_%d_%d" % (w, t), align_bytes=64)
+            scales = keep.tile([P, PASSES * P], U8, name="x_scales_%d_%d" % (w, t), align_bytes=64)
+            x_codes[(w, t)] = (codes, scales)
+            return (grouped[:], codes[:], scales[:])
+
+        def project(w, kind, h):
+            bank = psum.tile([P, TOKEN_TILES, HEAD_DIM], F32, tag="bank")
+            columns = slice(h * HEAD_DIM, (h + 1) * HEAD_DIM)
+            for t in range(TOKEN_TILES):
+                codes, scales = x_codes[(w, t)]
+                for g in range(PASSES):
+                    tokens = slice(g * P, (g + 1) * P)
+                    nc.tensor.matmul_mx(
+                        out=bank[:, t, :],
+                        lhsT=codes[:, tokens].bitcast(FP8X4),
+                        lhsT_scale=scales[:, tokens],
+                        rhs=w_codes[kind][:, g, columns].bitcast(FP8X4),
+                        rhs_scale=w_planes[4 * (PASSES * kind + g) : P, columns],
+                        start=(g == 0),
+                        stop=(g == PASSES - 1),
+                    )
+            return bank[:].rearrange("p t c -> p c t")
+
+        head_codes = {}
+
+        def context(group):
+            bank = psum.tile([P, GROUP, HEAD_DIM], F32, tag="bank")
+            for i in range(GROUP):
+                codes, scales = head_codes[group * GROUP + i]
+                nc.tensor.matmul_mx(
+                    out=bank[:, i, :],
+                    lhsT=codes[:, KEYS, :].bitcast(FP8X4),
+                    lhsT_scale=scales[:, KEYS, :],
+                    rhs=codes[:, VALUES, :].bitcast(FP8X4),
+                    rhs_scale=scales[:, VALUES, :],
+                    start=True,
+                    stop=True,
+                )
+            result = store_pool.tile([P, GROUP, HEAD_DIM], F32, tag="result")
+            nc.scalar.copy(out=result[:], in_=bank[:])
+            w, first_head = divmod(group * GROUP, HEADS)
+            nc.sync.dma_start(
+                out=out[w, first_head : first_head + GROUP].rearrange("h d e -> d h e"),
+                in_=result[:],
+            )
+
+        for t in range(TOKEN_TILES):
+            quantise(*transpose_x(0, t))
+
+        waiting = []
+        for step in range(WINDOWS * HEADS):
+            w, h = divmod(step, HEADS)
+            k_bank = project(w, KEYS, h)
+            v_bank = project(w, VALUES, h)
+
+            grouped = stage.tile([P, 2, HEAD_DIM, PACK], BF16, align_bytes=64, tag="kv_grouped")
+            exp_k = stage.tile([P, HEAD_DIM, PACK], F32, tag="exp_k")
+            nc.scalar.activation(out=exp_k[:], in_=k_bank, func=ACT.Exp)
+            nc.scalar.copy(out=grouped[:, VALUES], in_=v_bank)
+            nc.vector.tensor_scalar_min(out=exp_k[:], in0=exp_k[:], scalar1=1.0)
+            for job in waiting:
+                quantise(*job)
+            nc.vector.scalar_tensor_tensor(
+                out=grouped[:, KEYS],
+                in0=k_bank,
+                scalar=0.0,
+                in1=exp_k[:],
+                op0=ALU.max,
+                op1=ALU.add,
+            )
+            codes = head_codes_pool.tile([P, 2, HEAD_DIM], U32, align_bytes=64, tag="kv_codes")
+            scales = head_codes_pool.tile([P, 2, HEAD_DIM], U8, align_bytes=64, tag="kv_scales")
+            head_codes[step] = (codes, scales)
+            waiting = [
+                (
+                    grouped[:].rearrange("p k c t -> p (k c t)"),
+                    codes[:].rearrange("p k c -> p (k c)"),
+                    scales[:].rearrange("p k c -> p (k c)"),
+                )
+            ]
+
+            if w + 1 < WINDOWS and h in X_AHEAD:
+                half = X_AHEAD.index(h)
+                waiting.append(transpose_x(w + 1, 2 * half))
+                waiting.append(transpose_x(w + 1, 2 * half + 1))
+
+            newest = step - CONTEXT_LAG
+            if newest >= 0 and newest % GROUP == GROUP - 1:
+                context(newest // GROUP)
+
+        for job in waiting:
+            quantise(*job)
+        context(WINDOWS * HEADS // GROUP - 1)

@@ -23,8 +23,9 @@ HEADS = 8
 HEAD_DIM = 128
 INNER = HEADS * HEAD_DIM
 KEYS, VALUES = 0, 1
-GROUP = 4
-CONTEXT_LAG = 2
+LOAD_HEADS = 4
+GROUP = 2
+CONTEXT_LAG = 5
 X_AHEAD = (3, 5)
 
 FLOPS = 2 * 2 * WINDOWS * 512 * FEATURES * INNER + 2 * WINDOWS * HEADS * 512 * HEAD_DIM * HEAD_DIM
@@ -38,7 +39,7 @@ def tile_localcontextprocessor_pa_kernel(
         stack.enter_context(tc.manual_schedule())
         keep = stack.enter_context(tc.tile_pool(name="keep", bufs=1))
         x_stage = stack.enter_context(tc.tile_pool(name="x_stage", bufs=4))
-        stage = stack.enter_context(tc.tile_pool(name="stage", bufs=3))
+        stage = stack.enter_context(tc.tile_pool(name="stage", bufs=4))
         head_codes_pool = stack.enter_context(tc.tile_pool(name="head_codes", bufs=8))
         store_pool = stack.enter_context(tc.tile_pool(name="store", bufs=2))
         psum = stack.enter_context(tc.psum_pool(name="psum", bufs=8))
@@ -56,10 +57,10 @@ def tile_localcontextprocessor_pa_kernel(
         x_sb = {}
 
         def load_x(w):
-            for half in range(2):
-                x_pair = keep.tile([P, 2, FEATURES], BF16, name="x_pair_%d_%d" % (w, half))
-                nc.sync.dma_start(out=x_pair[:], in_=x_rows[w][:, 2 * half : 2 * half + 2, :])
-                x_sb[(w, half)] = x_pair
+            for t in range(TOKEN_TILES):
+                x_tile = keep.tile([P, FEATURES], BF16, name="x_tile_%d_%d" % (w, t))
+                nc.sync.dma_start(out=x_tile[:], in_=x_rows[w][:, t, :])
+                x_sb[(w, t)] = x_tile
 
         w_codes = {
             KEYS: keep.tile([P, PASSES, INNER], U32, name="w_k_codes", align_bytes=64),
@@ -77,8 +78,8 @@ def tile_localcontextprocessor_pa_kernel(
                 )
 
         def load_codes(kind, group):
-            first = group * GROUP * HEAD_DIM
-            last = first + GROUP * HEAD_DIM
+            first = group * LOAD_HEADS * HEAD_DIM
+            last = first + LOAD_HEADS * HEAD_DIM
             code_bytes = w_words[kind].rearrange("g p n t -> p g (n t)")
             nc.sync.dma_start(
                 out=w_codes[kind][:, :, first:last].bitcast(I32),
@@ -100,7 +101,7 @@ def tile_localcontextprocessor_pa_kernel(
             nc.vector.quantize_mx(out=codes.bitcast(FP8X4), scales=scales, in_=grouped)
 
         def transpose_x(w, t):
-            words = x_sb[(w, t // 2)][:, t % 2, :].bitcast(F32)
+            words = x_sb[(w, t)][:].bitcast(F32)
             flipped = psum.tile([P, PASSES, HALF_WORDS, P], F32, tag="bank")
             for g in range(PASSES):
                 for u in range(HALF_WORDS):
@@ -110,7 +111,7 @@ def tile_localcontextprocessor_pa_kernel(
                         identity[:],
                     )
             grouped = x_stage.tile([P, PASSES * P * PACK], BF16, align_bytes=64, tag="x_grouped")
-            copy = nc.vector.tensor_copy if t % 2 == 0 else nc.scalar.copy
+            copy = nc.vector.tensor_copy if (w == 0 and t % 2 == 0) else nc.scalar.copy
             copy(
                 out=grouped[:].bitcast(F32).rearrange(
                     "p (g r u) -> p g r u", g=PASSES, u=HALF_WORDS
@@ -166,47 +167,51 @@ def tile_localcontextprocessor_pa_kernel(
         for t in range(TOKEN_TILES):
             quantise(*transpose_x(0, t))
 
+        all_heads = WINDOWS * HEADS
+        grouped = {}
         waiting = []
-        for step in range(WINDOWS * HEADS):
-            w, h = divmod(step, HEADS)
-            k_bank = project(w, KEYS, h)
-            v_bank = project(w, VALUES, h)
+        for step in range(all_heads + CONTEXT_LAG):
+            if step < all_heads:
+                w, h = divmod(step, HEADS)
+                k_bank = project(w, KEYS, h)
+                grouped[step] = stage.tile(
+                    [P, 2, HEAD_DIM, PACK], BF16, align_bytes=64, name="kv_grouped", tag="kv_grouped"
+                )
+                exp_k = stage.tile([P, HEAD_DIM, PACK], F32, tag="exp_k")
+                nc.scalar.activation(out=exp_k[:], in_=k_bank, func=ACT.Exp)
+                nc.vector.tensor_scalar_min(out=exp_k[:], in0=exp_k[:], scalar1=1.0)
 
-            grouped = stage.tile([P, 2, HEAD_DIM, PACK], BF16, align_bytes=64, tag="kv_grouped")
-            exp_k = stage.tile([P, HEAD_DIM, PACK], F32, tag="exp_k")
-            nc.scalar.activation(out=exp_k[:], in_=k_bank, func=ACT.Exp)
-            nc.scalar.copy(out=grouped[:, VALUES], in_=v_bank)
-            nc.vector.tensor_scalar_min(out=exp_k[:], in0=exp_k[:], scalar1=1.0)
+            if 0 <= step - 1 < all_heads:
+                v_bank = project((step - 1) // HEADS, VALUES, (step - 1) % HEADS)
+                nc.scalar.copy(out=grouped[step - 1][:, VALUES], in_=v_bank)
+
             for job in waiting:
                 quantise(*job)
-            nc.vector.scalar_tensor_tensor(
-                out=grouped[:, KEYS],
-                in0=k_bank,
-                scalar=0.0,
-                in1=exp_k[:],
-                op0=ALU.max,
-                op1=ALU.add,
-            )
-            codes = head_codes_pool.tile([P, 2, HEAD_DIM], U32, align_bytes=64, tag="kv_codes")
-            scales = head_codes_pool.tile([P, 2, HEAD_DIM], U8, align_bytes=64, tag="kv_scales")
-            head_codes[step] = (codes, scales)
-            waiting = [
-                (
-                    grouped[:].rearrange("p k c t -> p (k c t)"),
+            waiting = []
+            if 0 <= step - 2 < all_heads:
+                codes = head_codes_pool.tile([P, 2, HEAD_DIM], U32, align_bytes=64, tag="kv_codes")
+                scales = head_codes_pool.tile([P, 2, HEAD_DIM], U8, align_bytes=64, tag="kv_scales")
+                head_codes[step - 2] = (codes, scales)
+                quantise(
+                    grouped[step - 2][:].rearrange("p k c t -> p (k c t)"),
                     codes[:].rearrange("p k c -> p (k c)"),
                     scales[:].rearrange("p k c -> p (k c)"),
                 )
-            ]
 
-            if w + 1 < WINDOWS and h in X_AHEAD:
-                half = X_AHEAD.index(h)
-                waiting.append(transpose_x(w + 1, 2 * half))
-                waiting.append(transpose_x(w + 1, 2 * half + 1))
+            if step < all_heads:
+                nc.vector.scalar_tensor_tensor(
+                    out=grouped[step][:, KEYS],
+                    in0=k_bank,
+                    scalar=0.0,
+                    in1=exp_k[:],
+                    op0=ALU.max,
+                    op1=ALU.add,
+                )
+                if w + 1 < WINDOWS and h in X_AHEAD:
+                    half = X_AHEAD.index(h)
+                    waiting.append(transpose_x(w + 1, 2 * half))
+                    waiting.append(transpose_x(w + 1, 2 * half + 1))
 
             newest = step - CONTEXT_LAG
             if newest >= 0 and newest % GROUP == GROUP - 1:
                 context(newest // GROUP)
-
-        for job in waiting:
-            quantise(*job)
-        context(WINDOWS * HEADS // GROUP - 1)

@@ -25,7 +25,8 @@ INNER = HEADS * HEAD_DIM
 KEYS, VALUES = 0, 1
 LOAD_HEADS = 4
 GROUP = 2
-CONTEXT_LAG = 5
+SKEW = 3
+CONTEXT_LAG = SKEW + 3
 X_AHEAD = (3, 5)
 
 FLOPS = 2 * 2 * WINDOWS * 512 * FEATURES * INNER + 2 * WINDOWS * HEADS * 512 * HEAD_DIM * HEAD_DIM
@@ -39,7 +40,8 @@ def tile_localcontextprocessor_pa_kernel(
         stack.enter_context(tc.manual_schedule())
         keep = stack.enter_context(tc.tile_pool(name="keep", bufs=1))
         x_stage = stack.enter_context(tc.tile_pool(name="x_stage", bufs=4))
-        stage = stack.enter_context(tc.tile_pool(name="stage", bufs=4))
+        exp_pool = stack.enter_context(tc.tile_pool(name="exp", bufs=3))
+        grouped_pool = stack.enter_context(tc.tile_pool(name="grouped", bufs=SKEW + 3))
         head_codes_pool = stack.enter_context(tc.tile_pool(name="head_codes", bufs=8))
         store_pool = stack.enter_context(tc.tile_pool(name="store", bufs=2))
         psum = stack.enter_context(tc.psum_pool(name="psum", bufs=8))
@@ -111,7 +113,7 @@ def tile_localcontextprocessor_pa_kernel(
                         identity[:],
                     )
             grouped = x_stage.tile([P, PASSES * P * PACK], BF16, align_bytes=64, tag="x_grouped")
-            copy = nc.vector.tensor_copy if (w == 0 and t % 2 == 0) else nc.scalar.copy
+            copy = nc.vector.tensor_copy if t % 2 == 0 else nc.scalar.copy
             copy(
                 out=grouped[:].bitcast(F32).rearrange(
                     "p (g r u) -> p g r u", g=PASSES, u=HALF_WORDS
@@ -174,26 +176,28 @@ def tile_localcontextprocessor_pa_kernel(
             if step < all_heads:
                 w, h = divmod(step, HEADS)
                 k_bank = project(w, KEYS, h)
-                grouped[step] = stage.tile(
+                grouped[step] = grouped_pool.tile(
                     [P, 2, HEAD_DIM, PACK], BF16, align_bytes=64, name="kv_grouped", tag="kv_grouped"
                 )
-                exp_k = stage.tile([P, HEAD_DIM, PACK], F32, tag="exp_k")
+                exp_k = exp_pool.tile([P, HEAD_DIM, PACK], BF16, tag="exp_k")
                 nc.scalar.activation(out=exp_k[:], in_=k_bank, func=ACT.Exp)
                 nc.vector.tensor_scalar_min(out=exp_k[:], in0=exp_k[:], scalar1=1.0)
 
-            if 0 <= step - 1 < all_heads:
-                v_bank = project((step - 1) // HEADS, VALUES, (step - 1) % HEADS)
-                nc.scalar.copy(out=grouped[step - 1][:, VALUES], in_=v_bank)
+            v_head = step - SKEW
+            if 0 <= v_head < all_heads:
+                v_bank = project(v_head // HEADS, VALUES, v_head % HEADS)
+                nc.scalar.copy(out=grouped[v_head][:, VALUES], in_=v_bank)
 
             for job in waiting:
                 quantise(*job)
             waiting = []
-            if 0 <= step - 2 < all_heads:
+            full_head = step - SKEW - 1
+            if 0 <= full_head < all_heads:
                 codes = head_codes_pool.tile([P, 2, HEAD_DIM], U32, align_bytes=64, tag="kv_codes")
                 scales = head_codes_pool.tile([P, 2, HEAD_DIM], U8, align_bytes=64, tag="kv_scales")
-                head_codes[step - 2] = (codes, scales)
+                head_codes[full_head] = (codes, scales)
                 quantise(
-                    grouped[step - 2][:].rearrange("p k c t -> p (k c t)"),
+                    grouped[full_head][:].rearrange("p k c t -> p (k c t)"),
                     codes[:].rearrange("p k c -> p (k c)"),
                     scales[:].rearrange("p k c -> p (k c)"),
                 )

@@ -23,11 +23,10 @@ HEADS = 8
 HEAD_DIM = 128
 INNER = HEADS * HEAD_DIM
 KEYS, VALUES = 0, 1
-LOAD_HEADS = 4
 GROUP = 2
 SKEW = 3
 CONTEXT_LAG = SKEW + 3
-X_AHEAD = (3, 5)
+X_AHEAD = 1
 
 FLOPS = 2 * 2 * WINDOWS * 512 * FEATURES * INNER + 2 * WINDOWS * HEADS * 512 * HEAD_DIM * HEAD_DIM
 
@@ -43,11 +42,15 @@ def tile_localcontextprocessor_pa_kernel(
         exp_pool = stack.enter_context(tc.tile_pool(name="exp", bufs=3))
         grouped_pool = stack.enter_context(tc.tile_pool(name="grouped", bufs=SKEW + 3))
         head_codes_pool = stack.enter_context(tc.tile_pool(name="head_codes", bufs=8))
-        store_pool = stack.enter_context(tc.tile_pool(name="store", bufs=2))
+        store_pool = stack.enter_context(tc.tile_pool(name="store", bufs=8))
         psum = stack.enter_context(tc.psum_pool(name="psum", bufs=8))
 
-        w_planes = keep.tile([P, INNER], U8, align_bytes=64)
-        nc.vector.memset(w_planes[:].bitcast(I32), 0)
+        w_planes = {
+            KEYS: keep.tile([P, INNER], U8, name="w_k_planes", align_bytes=64),
+            VALUES: keep.tile([P, INNER], U8, name="w_v_planes", align_bytes=64),
+        }
+        for kind in (KEYS, VALUES):
+            nc.vector.memset(w_planes[kind][:].bitcast(I32), 0)
         zero = keep.tile([P, 1], F32)
         one = keep.tile([P, 1], F32)
         nc.vector.memset(zero[:], 0.0)
@@ -73,15 +76,15 @@ def tile_localcontextprocessor_pa_kernel(
 
         def load_scales(kind):
             for quadrant in range(4):
-                first = 32 * quadrant + 4 * PASSES * kind
+                first = 32 * quadrant
                 nc.sync.dma_start(
-                    out=w_planes[first : first + 4 * PASSES, :].bitcast(I32),
+                    out=w_planes[kind][first : first + 4 * PASSES, :].bitcast(I32),
                     in_=w_scales[kind][:, 4 * quadrant : 4 * quadrant + 4, :].bitcast(I32),
                 )
 
-        def load_codes(kind, group):
-            first = group * LOAD_HEADS * HEAD_DIM
-            last = first + LOAD_HEADS * HEAD_DIM
+        def load_codes(kind, first_head, heads):
+            first = first_head * HEAD_DIM
+            last = first + heads * HEAD_DIM
             code_bytes = w_words[kind].rearrange("g p n t -> p g (n t)")
             nc.sync.dma_start(
                 out=w_codes[kind][:, :, first:last].bitcast(I32),
@@ -90,12 +93,14 @@ def tile_localcontextprocessor_pa_kernel(
 
         load_x(0)
         load_scales(KEYS)
-        load_codes(KEYS, 0)
-        load_codes(VALUES, 0)
-        load_scales(VALUES)
+        load_codes(KEYS, 0, 2)
         load_x(1)
-        load_codes(KEYS, 1)
-        load_codes(VALUES, 1)
+        load_codes(KEYS, 2, 2)
+        load_scales(VALUES)
+        load_codes(VALUES, 0, 2)
+        load_codes(VALUES, 2, 2)
+        load_codes(KEYS, 4, 4)
+        load_codes(VALUES, 4, 4)
 
         x_codes = {}
 
@@ -137,7 +142,7 @@ def tile_localcontextprocessor_pa_kernel(
                         lhsT=codes[:, tokens].bitcast(FP8X4),
                         lhsT_scale=scales[:, tokens],
                         rhs=w_codes[kind][:, g, columns].bitcast(FP8X4),
-                        rhs_scale=w_planes[4 * (PASSES * kind + g) : P, columns],
+                        rhs_scale=w_planes[kind][4 * g : P, columns],
                         start=(g == 0),
                         stop=(g == PASSES - 1),
                     )
@@ -145,10 +150,10 @@ def tile_localcontextprocessor_pa_kernel(
 
         head_codes = {}
 
-        def context(group):
-            bank = psum.tile([P, GROUP, HEAD_DIM], F32, tag="bank")
-            for i in range(GROUP):
-                codes, scales = head_codes[group * GROUP + i]
+        def context(first, heads, copy):
+            bank = psum.tile([P, heads, HEAD_DIM], F32, tag="bank")
+            for i in range(heads):
+                codes, scales = head_codes[first + i]
                 nc.tensor.matmul_mx(
                     out=bank[:, i, :],
                     lhsT=codes[:, KEYS, :].bitcast(FP8X4),
@@ -158,11 +163,11 @@ def tile_localcontextprocessor_pa_kernel(
                     start=True,
                     stop=True,
                 )
-            result = store_pool.tile([P, GROUP, HEAD_DIM], F32, tag="result")
-            nc.scalar.copy(out=result[:], in_=bank[:])
-            w, first_head = divmod(group * GROUP, HEADS)
+            result = store_pool.tile([P, heads, HEAD_DIM], F32, tag="result")
+            copy(out=result[:], in_=bank[:])
+            w, h = divmod(first, HEADS)
             nc.sync.dma_start(
-                out=out[w, first_head : first_head + GROUP].rearrange("h d e -> d h e"),
+                out=out[w, h : h + heads].rearrange("h d e -> d h e"),
                 in_=result[:],
             )
 
@@ -172,7 +177,7 @@ def tile_localcontextprocessor_pa_kernel(
         all_heads = WINDOWS * HEADS
         grouped = {}
         waiting = []
-        for step in range(all_heads + CONTEXT_LAG):
+        for step in range(all_heads + SKEW + 2):
             if step < all_heads:
                 w, h = divmod(step, HEADS)
                 k_bank = project(w, KEYS, h)
@@ -196,11 +201,13 @@ def tile_localcontextprocessor_pa_kernel(
                 codes = head_codes_pool.tile([P, 2, HEAD_DIM], U32, align_bytes=64, tag="kv_codes")
                 scales = head_codes_pool.tile([P, 2, HEAD_DIM], U8, align_bytes=64, tag="kv_scales")
                 head_codes[full_head] = (codes, scales)
-                quantise(
-                    grouped[full_head][:].rearrange("p k c t -> p (k c t)"),
-                    codes[:].rearrange("p k c -> p (k c)"),
-                    scales[:].rearrange("p k c -> p (k c)"),
-                )
+                kinds = (slice(0, 1), slice(1, 2)) if full_head == all_heads - 1 else (slice(0, 2),)
+                for kind in kinds:
+                    quantise(
+                        grouped[full_head][:, kind].rearrange("p k c t -> p (k c t)"),
+                        codes[:, kind].rearrange("p k c -> p (k c)"),
+                        scales[:, kind].rearrange("p k c -> p (k c)"),
+                    )
 
             if step < all_heads:
                 nc.vector.scalar_tensor_tensor(
@@ -211,11 +218,13 @@ def tile_localcontextprocessor_pa_kernel(
                     op0=ALU.max,
                     op1=ALU.add,
                 )
-                if w + 1 < WINDOWS and h in X_AHEAD:
-                    half = X_AHEAD.index(h)
-                    waiting.append(transpose_x(w + 1, 2 * half))
-                    waiting.append(transpose_x(w + 1, 2 * half + 1))
+                if step == X_AHEAD:
+                    for t in range(TOKEN_TILES):
+                        waiting.append(transpose_x(1, t))
 
             newest = step - CONTEXT_LAG
-            if newest >= 0 and newest % GROUP == GROUP - 1:
-                context(newest // GROUP)
+            if 0 <= newest < all_heads - GROUP and newest % GROUP == GROUP - 1:
+                copy = nc.vector.tensor_copy if step < all_heads + SKEW else nc.scalar.copy
+                context(newest + 1 - GROUP, GROUP, copy)
+        context(all_heads - 2, 1, nc.scalar.copy)
+        context(all_heads - 1, 1, nc.vector.tensor_copy)

@@ -28,6 +28,10 @@ SKEW = 3
 CONTEXT_LAG = SKEW + 3
 X_AHEAD = 1
 
+IDLE_COLUMNS = 512
+IDLE_BEFORE_X = 4
+IDLE_BEHIND_X = 2
+
 FLOPS = 2 * 2 * WINDOWS * 512 * FEATURES * INNER + 2 * WINDOWS * HEADS * 512 * HEAD_DIM * HEAD_DIM
 
 
@@ -45,18 +49,28 @@ def tile_localcontextprocessor_pa_kernel(
         store_pool = stack.enter_context(tc.tile_pool(name="store", bufs=8))
         psum = stack.enter_context(tc.psum_pool(name="psum", bufs=8))
 
-        w_planes = {
-            KEYS: keep.tile([P, INNER], U8, name="w_k_planes", align_bytes=64),
-            VALUES: keep.tile([P, INNER], U8, name="w_v_planes", align_bytes=64),
-        }
-        for kind in (KEYS, VALUES):
-            nc.vector.memset(w_planes[kind][:].bitcast(I32), 0)
+        idle_zeros = keep.tile([P, IDLE_COLUMNS], BF16)
+        nc.vector.memset(idle_zeros[:], 0.0)
+
+        def idle_matmuls(count):
+            bank = psum.tile([P, IDLE_COLUMNS], F32, name="idle_bank", tag="bank")
+            for i in range(count):
+                nc.tensor.matmul(
+                    bank[:], lhsT=idle_zeros[:, :P], rhs=idle_zeros[:], start=True, stop=True
+                )
+
         zero = keep.tile([P, 1], F32)
         one = keep.tile([P, 1], F32)
         nc.vector.memset(zero[:], 0.0)
         nc.scalar.activation(out=one[:], in_=zero[:], func=ACT.Exp)
         identity = keep.tile([P, P], F32)
         masks.make_identity(nc, identity[:])
+        w_planes = {
+            KEYS: keep.tile([P, INNER], U8, name="w_k_planes", align_bytes=64),
+            VALUES: keep.tile([P, INNER], U8, name="w_v_planes", align_bytes=64),
+        }
+        for kind in (KEYS, VALUES):
+            nc.vector.memset(w_planes[kind][:].bitcast(I32), 0)
 
         x_rows = x[0].rearrange("(w p t) d -> w p t d", w=WINDOWS, t=TOKEN_TILES)
         x_sb = {}
@@ -171,8 +185,10 @@ def tile_localcontextprocessor_pa_kernel(
                 in_=result[:],
             )
 
+        idle_matmuls(IDLE_BEFORE_X)
         for t in range(TOKEN_TILES):
             quantise(*transpose_x(0, t))
+        idle_matmuls(IDLE_BEHIND_X)
 
         all_heads = WINDOWS * HEADS
         grouped = {}

@@ -240,7 +240,6 @@ def tile_localcontextprocessor_pa_kernel(
 
             newest = step - CONTEXT_LAG
             if 0 <= newest < all_heads - GROUP and newest % GROUP == GROUP - 1:
-                copy = nc.vector.tensor_copy if step < all_heads + SKEW else nc.scalar.copy
-                context(newest + 1 - GROUP, GROUP, copy)
+                context(newest + 1 - GROUP, GROUP, nc.scalar.copy)
         context(all_heads - 2, 1, nc.scalar.copy)
         context(all_heads - 1, 1, nc.vector.tensor_copy)

@@ -26,7 +26,8 @@ KEYS, VALUES = 0, 1
 GROUP = 2
 SKEW = 3
 CONTEXT_LAG = SKEW + 3
-X_AHEAD = 1
+FIRST_HEADS = 2
+X_AHEAD = FIRST_HEADS - 1
 
 IDLE_COLUMNS = 512
 IDLE_BEFORE_X = 4
@@ -112,8 +113,9 @@ def tile_localcontextprocessor_pa_kernel(
         load_codes(KEYS, 2, 2)
         load_scales(VALUES)
         load_codes(VALUES, 0, 2)
+        load_codes(KEYS, 4, 2)
         load_codes(VALUES, 2, 2)
-        load_codes(KEYS, 4, 4)
+        load_codes(KEYS, 6, 2)
         load_codes(VALUES, 4, 4)
 
         x_codes = {}
@@ -144,10 +146,9 @@ def tile_localcontextprocessor_pa_kernel(
             x_codes[(w, t)] = (codes, scales)
             return (grouped[:], codes[:], scales[:])
 
-        def project(w, kind, h):
-            bank = psum.tile([P, TOKEN_TILES, HEAD_DIM], F32, tag="bank")
+        def project_tiles(bank, w, kind, h, tiles):
             columns = slice(h * HEAD_DIM, (h + 1) * HEAD_DIM)
-            for t in range(TOKEN_TILES):
+            for t in tiles:
                 codes, scales = x_codes[(w, t)]
                 for g in range(PASSES):
                     tokens = slice(g * P, (g + 1) * P)
@@ -160,7 +161,16 @@ def tile_localcontextprocessor_pa_kernel(
                         start=(g == 0),
                         stop=(g == PASSES - 1),
                     )
-            return bank[:].rearrange("p t c -> p c t")
+
+        def project(w, kind, heads):
+            banks = []
+            for h in heads:
+                bank = psum.tile([P, TOKEN_TILES, HEAD_DIM], F32, name="bank", tag="bank")
+                banks.append(bank)
+            for tiles in (range(TOKEN_TILES - 1), range(TOKEN_TILES - 1, TOKEN_TILES)):
+                for bank, h in zip(banks, heads):
+                    project_tiles(bank, w, kind, h, tiles)
+            return [bank[:].rearrange("p t c -> p c t") for bank in banks]
 
         head_codes = {}
 
@@ -192,11 +202,16 @@ def tile_localcontextprocessor_pa_kernel(
 
         all_heads = WINDOWS * HEADS
         grouped = {}
+        k_banks = []
         waiting = []
         for step in range(all_heads + SKEW + 2):
             if step < all_heads:
                 w, h = divmod(step, HEADS)
-                k_bank = project(w, KEYS, h)
+                if step == 0:
+                    k_banks.extend(project(w, KEYS, range(FIRST_HEADS)))
+                elif step >= FIRST_HEADS:
+                    k_banks.extend(project(w, KEYS, [h]))
+                k_bank = k_banks[step]
                 grouped[step] = grouped_pool.tile(
                     [P, 2, HEAD_DIM, PACK], BF16, align_bytes=64, name="kv_grouped", tag="kv_grouped"
                 )
@@ -206,7 +221,7 @@ def tile_localcontextprocessor_pa_kernel(
 
             v_head = step - SKEW
             if 0 <= v_head < all_heads:
-                v_bank = project(v_head // HEADS, VALUES, v_head % HEADS)
+                v_bank = project(v_head // HEADS, VALUES, [v_head % HEADS])[0]
                 nc.scalar.copy(out=grouped[v_head][:, VALUES], in_=v_bank)
 
             for job in waiting:

@@ -27,7 +27,7 @@ GROUP = 2
 SKEW = 3
 CONTEXT_LAG = SKEW + 3
 FIRST_HEADS = 2
-X_AHEAD = FIRST_HEADS - 1
+X_AHEAD = (1, 2)
 
 IDLE_COLUMNS = 512
 IDLE_BEFORE_X = 4
@@ -76,8 +76,8 @@ def tile_localcontextprocessor_pa_kernel(
         x_rows = x[0].rearrange("(w p t) d -> w p t d", w=WINDOWS, t=TOKEN_TILES)
         x_sb = {}
 
-        def load_x(w):
-            for t in range(TOKEN_TILES):
+        def load_x(w, tiles):
+            for t in tiles:
                 x_tile = keep.tile([P, FEATURES], BF16, name="x_tile_%d_%d" % (w, t))
                 nc.sync.dma_start(out=x_tile[:], in_=x_rows[w][:, t, :])
                 x_sb[(w, t)] = x_tile
@@ -106,11 +106,12 @@ def tile_localcontextprocessor_pa_kernel(
                 in_=code_bytes[:, :, PACK * first : PACK * last].bitcast(I32),
             )
 
-        load_x(0)
+        load_x(0, range(TOKEN_TILES))
         load_scales(KEYS)
         load_codes(KEYS, 0, 2)
-        load_x(1)
+        load_x(1, range(0, 2))
         load_codes(KEYS, 2, 2)
+        load_x(1, range(2, 4))
         load_scales(VALUES)
         load_codes(VALUES, 0, 2)
         load_codes(KEYS, 4, 2)
@@ -249,12 +250,14 @@ def tile_localcontextprocessor_pa_kernel(
                     op0=ALU.max,
                     op1=ALU.add,
                 )
-                if step == X_AHEAD:
-                    for t in range(TOKEN_TILES):
-                        waiting.append(transpose_x(1, t))
+                if step in X_AHEAD:
+                    half = X_AHEAD.index(step)
+                    waiting.append(transpose_x(1, 2 * half))
+                    waiting.append(transpose_x(1, 2 * half + 1))
 
             newest = step - CONTEXT_LAG
             if 0 <= newest < all_heads - GROUP and newest % GROUP == GROUP - 1:
-                context(newest + 1 - GROUP, GROUP, nc.scalar.copy)
+                turn = newest // GROUP % 2
+                context(newest + 1 - GROUP, GROUP, nc.scalar.copy if turn else nc.vector.tensor_copy)
         context(all_heads - 2, 1, nc.scalar.copy)
         context(all_heads - 1, 1, nc.vector.tensor_copy)

@@ -126,26 +126,34 @@ def tile_localcontextprocessor_pa_kernel(
 
         def transpose_x(w, t):
             words = x_sb[(w, t)][:].bitcast(F32)
-            flipped = psum.tile([P, PASSES, HALF_WORDS, P], F32, tag="bank")
-            for g in range(PASSES):
-                for u in range(HALF_WORDS):
-                    nc.tensor.transpose(
-                        flipped[:, g, u, :],
-                        words[:, 256 * g + u : 256 * (g + 1) : HALF_WORDS],
-                        identity[:],
-                    )
             grouped = x_stage.tile([P, PASSES * P * PACK], BF16, align_bytes=64, tag="x_grouped")
-            copy = nc.vector.tensor_copy if t % 2 == 0 else nc.scalar.copy
-            copy(
-                out=grouped[:].bitcast(F32).rearrange(
-                    "p (g r u) -> p g r u", g=PASSES, u=HALF_WORDS
-                ),
-                in_=flipped[:].rearrange("p g u r -> p g r u"),
-            )
             codes = keep.tile([P, PASSES * P], U32, name="x_codes_%d_%d" % (w, t), align_bytes=64)
             scales = keep.tile([P, PASSES * P], U8, name="x_scales_%d_%d" % (w, t), align_bytes=64)
             x_codes[(w, t)] = (codes, scales)
-            return (grouped[:], codes[:], scales[:])
+            if w == 0:
+                parts = [(0, 1, nc.vector.tensor_copy), (1, 2, nc.scalar.copy)]
+            else:
+                parts = [(0, PASSES, nc.scalar.copy)]
+            jobs = []
+            for first, last, copy in parts:
+                flipped = psum.tile([P, last - first, HALF_WORDS, P], F32, name="flipped", tag="bank")
+                for g in range(first, last):
+                    for u in range(HALF_WORDS):
+                        nc.tensor.transpose(
+                            flipped[:, g - first, u, :],
+                            words[:, 256 * g + u : 256 * (g + 1) : HALF_WORDS],
+                            identity[:],
+                        )
+                values = grouped[:, first * P * PACK : last * P * PACK]
+                copy(
+                    out=values.bitcast(F32).rearrange(
+                        "p (g r u) -> p g r u", g=last - first, u=HALF_WORDS
+                    ),
+                    in_=flipped[:].rearrange("p g u r -> p g r u"),
+                )
+                tokens = slice(first * P, last * P)
+                jobs.append((values, codes[:, tokens], scales[:, tokens]))
+            return jobs
 
         def project_tiles(bank, w, kind, h, tiles):
             columns = slice(h * HEAD_DIM, (h + 1) * HEAD_DIM)
@@ -198,7 +206,8 @@ def tile_localcontextprocessor_pa_kernel(
 
         idle_matmuls(IDLE_BEFORE_X)
         for t in range(TOKEN_TILES):
-            quantise(*transpose_x(0, t))
+            for job in transpose_x(0, t):
+                quantise(*job)
         idle_matmuls(IDLE_BEHIND_X)
 
         all_heads = WINDOWS * HEADS
@@ -252,12 +261,12 @@ def tile_localcontextprocessor_pa_kernel(
                 )
                 if step in X_AHEAD:
                     half = X_AHEAD.index(step)
-                    waiting.append(transpose_x(1, 2 * half))
-                    waiting.append(transpose_x(1, 2 * half + 1))
+                    for t in (2 * half, 2 * half + 1):
+                        waiting.extend(transpose_x(1, t))
 
             newest = step - CONTEXT_LAG
             if 0 <= newest < all_heads - GROUP and newest % GROUP == GROUP - 1:
-                turn = newest // GROUP % 2
+                turn = newest // GROUP % 2 or step >= all_heads
                 context(newest + 1 - GROUP, GROUP, nc.scalar.copy if turn else nc.vector.tensor_copy)
         context(all_heads - 2, 1, nc.scalar.copy)
         context(all_heads - 1, 1, nc.vector.tensor_copy)

from contextlib import ExitStack

import concourse.masks as masks
import concourse.mybir as mybir

F32 = mybir.dt.float32
BF16 = mybir.dt.bfloat16
I32 = mybir.dt.int32
U32 = mybir.dt.uint32
U8 = mybir.dt.uint8
FP8X4 = mybir.dt.float8_e4m3fn_x4
ACT = mybir.ActivationFunctionType
ALU = mybir.AluOpType

P = 128
PACK = 4
WINDOWS = 2
TOKEN_TILES = PACK
FEATURES = 1024
PASSES = FEATURES // (P * PACK)
HALF_WORDS = 2
HEADS = 8
HEAD_DIM = 128
INNER = HEADS * HEAD_DIM
KEYS, VALUES = 0, 1
GROUP = 2
SKEW = 3
CONTEXT_LAG = SKEW + 3
FIRST_HEADS = 2
X_AHEAD = (1, 2)

IDLE_COLUMNS = 512
IDLE_BEFORE_X = 4
IDLE_BEHIND_X = 2

FLOPS = 2 * 2 * WINDOWS * 512 * FEATURES * INNER + 2 * WINDOWS * HEADS * 512 * HEAD_DIM * HEAD_DIM


def tile_localcontextprocessor_pa_kernel(
    tc, x, w_k_words, w_k_scales, w_v_words, w_v_scales, out
):
    nc = tc.nc
    with ExitStack() as stack:
        stack.enter_context(tc.manual_schedule())
        keep = stack.enter_context(tc.tile_pool(name="keep", bufs=1))
        x_stage = stack.enter_context(tc.tile_pool(name="x_stage", bufs=4))
        exp_pool = stack.enter_context(tc.tile_pool(name="exp", bufs=3))
        grouped_pool = stack.enter_context(tc.tile_pool(name="grouped", bufs=SKEW + 3))
        head_codes_pool = stack.enter_context(tc.tile_pool(name="head_codes", bufs=8))
        store_pool = stack.enter_context(tc.tile_pool(name="store", bufs=8))
        psum = stack.enter_context(tc.psum_pool(name="psum", bufs=8))

        idle_zeros = keep.tile([P, IDLE_COLUMNS], BF16)
        nc.vector.memset(idle_zeros[:], 0.0)

        def idle_matmuls(count):
            bank = psum.tile([P, IDLE_COLUMNS], F32, name="idle_bank", tag="bank")
            for i in range(count):
                nc.tensor.matmul(
                    bank[:], lhsT=idle_zeros[:, :P], rhs=idle_zeros[:], start=True, stop=True
                )

        zero = keep.tile([P, 1], F32)
        one = keep.tile([P, 1], F32)
        nc.vector.memset(zero[:], 0.0)
        nc.scalar.activation(out=one[:], in_=zero[:], func=ACT.Exp)
        identity = keep.tile([P, P], F32)
        masks.make_identity(nc, identity[:])
        w_planes = {
            KEYS: keep.tile([P, INNER], U8, name="w_k_planes", align_bytes=64),
            VALUES: keep.tile([P, INNER], U8, name="w_v_planes", align_bytes=64),
        }
        for kind in (KEYS, VALUES):
            nc.vector.memset(w_planes[kind][:].bitcast(I32), 0)

        x_rows = x[0].rearrange("(w p t) d -> w p t d", w=WINDOWS, t=TOKEN_TILES)
        x_sb = {}

        def load_x(w, tiles):
            for t in tiles:
                x_tile = keep.tile([P, FEATURES], BF16, name="x_tile_%d_%d" % (w, t))
                nc.sync.dma_start(out=x_tile[:], in_=x_rows[w][:, t, :])
                x_sb[(w, t)] = x_tile

        w_codes = {
            KEYS: keep.tile([P, PASSES, INNER], U32, name="w_k_codes", align_bytes=64),
            VALUES: keep.tile([P, PASSES, INNER], U32, name="w_v_codes", align_bytes=64),
        }
        w_words = {KEYS: w_k_words, VALUES: w_v_words}
        w_scales = {KEYS: w_k_scales, VALUES: w_v_scales}

        def load_scales(kind):
            for quadrant in range(4):
                first = 32 * quadrant
                nc.sync.dma_start(
                    out=w_planes[kind][first : first + 4 * PASSES, :].bitcast(I32),
                    in_=w_scales[kind][:, 4 * quadrant : 4 * quadrant + 4, :].bitcast(I32),
                )

        def load_codes(kind, first_head, heads):
            first = first_head * HEAD_DIM
            last = first + heads * HEAD_DIM
            code_bytes = w_words[kind].rearrange("g p n t -> p g (n t)")
            nc.sync.dma_start(
                out=w_codes[kind][:, :, first:last].bitcast(I32),
                in_=code_bytes[:, :, PACK * first : PACK * last].bitcast(I32),
            )

        load_x(0, range(TOKEN_TILES))
        load_scales(KEYS)
        load_codes(KEYS, 0, 2)
        load_x(1, range(0, 2))
        load_codes(KEYS, 2, 2)
        load_x(1, range(2, 4))
        load_scales(VALUES)
        load_codes(VALUES, 0, 2)
        load_codes(KEYS, 4, 2)
        load_codes(VALUES, 2, 2)
        load_codes(KEYS, 6, 2)
        load_codes(VALUES, 4, 4)

        x_codes = {}

        def quantise(grouped, codes, scales):
            nc.vector.quantize_mx(out=codes.bitcast(FP8X4), scales=scales, in_=grouped)

        def transpose_x(w, t):
            words = x_sb[(w, t)][:].bitcast(F32)
            grouped = x_stage.tile([P, PASSES * P * PACK], BF16, align_bytes=64, tag="x_grouped")
            codes = keep.tile([P, PASSES * P], U32, name="x_codes_%d_%d" % (w, t), align_bytes=64)
            scales = keep.tile([P, PASSES * P], U8, name="x_scales_%d_%d" % (w, t), align_bytes=64)
            x_codes[(w, t)] = (codes, scales)
            if w == 0:
                parts = [(0, 1, nc.vector.tensor_copy), (1, 2, nc.scalar.copy)]
            else:
                parts = [(0, PASSES, nc.scalar.copy)]
            jobs = []
            for first, last, copy in parts:
                flipped = psum.tile([P, last - first, HALF_WORDS, P], F32, name="flipped", tag="bank")
                for g in range(first, last):
                    for u in range(HALF_WORDS):
                        nc.tensor.transpose(
                            flipped[:, g - first, u, :],
                            words[:, 256 * g + u : 256 * (g + 1) : HALF_WORDS],
                            identity[:],
                        )
                values = grouped[:, first * P * PACK : last * P * PACK]
                copy(
                    out=values.bitcast(F32).rearrange(
                        "p (g r u) -> p g r u", g=last - first, u=HALF_WORDS
                    ),
                    in_=flipped[:].rearrange("p g u r -> p g r u"),
                )
                tokens = slice(first * P, last * P)
                jobs.append((values, codes[:, tokens], scales[:, tokens]))
            return jobs

        def project_tiles(bank, w, kind, h, tiles):
            columns = slice(h * HEAD_DIM, (h + 1) * HEAD_DIM)
            for t in tiles:
                codes, scales = x_codes[(w, t)]
                for g in range(PASSES):
                    tokens = slice(g * P, (g + 1) * P)
                    nc.tensor.matmul_mx(
                        out=bank[:, t, :],
                        lhsT=codes[:, tokens].bitcast(FP8X4),
                        lhsT_scale=scales[:, tokens],
                        rhs=w_codes[kind][:, g, columns].bitcast(FP8X4),
                        rhs_scale=w_planes[kind][4 * g : P, columns],
                        start=(g == 0),
                        stop=(g == PASSES - 1),
                    )

        def project(w, kind, heads):
            banks = []
            for h in heads:
                bank = psum.tile([P, TOKEN_TILES, HEAD_DIM], F32, name="bank", tag="bank")
                banks.append(bank)
            for tiles in (range(TOKEN_TILES - 1), range(TOKEN_TILES - 1, TOKEN_TILES)):
                for bank, h in zip(banks, heads):
                    project_tiles(bank, w, kind, h, tiles)
            return [bank[:].rearrange("p t c -> p c t") for bank in banks]

        head_codes = {}

        def context(first, heads, copy):
            bank = psum.tile([P, heads, HEAD_DIM], F32, tag="bank")
            for i in range(heads):
                codes, scales = head_codes[first + i]
                nc.tensor.matmul_mx(
                    out=bank[:, i, :],
                    lhsT=codes[:, KEYS, :].bitcast(FP8X4),
                    lhsT_scale=scales[:, KEYS, :],
                    rhs=codes[:, VALUES, :].bitcast(FP8X4),
                    rhs_scale=scales[:, VALUES, :],
                    start=True,
                    stop=True,
                )
            result = store_pool.tile([P, heads, HEAD_DIM], F32, tag="result")
            copy(out=result[:], in_=bank[:])
            w, h = divmod(first, HEADS)
            nc.sync.dma_start(
                out=out[w, h : h + heads].rearrange("h d e -> d h e"),
                in_=result[:],
            )

        idle_matmuls(IDLE_BEFORE_X)
        for t in range(TOKEN_TILES):
            for job in transpose_x(0, t):
                quantise(*job)
        idle_matmuls(IDLE_BEHIND_X)

        all_heads = WINDOWS * HEADS
        grouped = {}
        k_banks = []
        waiting = []
        for step in range(all_heads + SKEW + 2):
            if step < all_heads:
                w, h = divmod(step, HEADS)
                if step == 0:
                    k_banks.extend(project(w, KEYS, range(FIRST_HEADS)))
                elif step >= FIRST_HEADS:
                    k_banks.extend(project(w, KEYS, [h]))
                k_bank = k_banks[step]
                grouped[step] = grouped_pool.tile(
                    [P, 2, HEAD_DIM, PACK], BF16, align_bytes=64, name="kv_grouped", tag="kv_grouped"
                )
                exp_k = exp_pool.tile([P, HEAD_DIM, PACK], BF16, tag="exp_k")
                nc.scalar.activation(out=exp_k[:], in_=k_bank, func=ACT.Exp)
                nc.vector.tensor_scalar_min(out=exp_k[:], in0=exp_k[:], scalar1=1.0)

            v_head = step - SKEW
            if 0 <= v_head < all_heads:
                v_bank = project(v_head // HEADS, VALUES, [v_head % HEADS])[0]
                nc.scalar.copy(out=grouped[v_head][:, VALUES], in_=v_bank)

            for job in waiting:
                quantise(*job)
            waiting = []
            full_head = step - SKEW - 1
            if 0 <= full_head < all_heads:
                codes = head_codes_pool.tile([P, 2, HEAD_DIM], U32, align_bytes=64, tag="kv_codes")
                scales = head_codes_pool.tile([P, 2, HEAD_DIM], U8, align_bytes=64, tag="kv_scales")
                head_codes[full_head] = (codes, scales)
                kinds = (slice(0, 1), slice(1, 2)) if full_head == all_heads - 1 else (slice(0, 2),)
                for kind in kinds:
                    quantise(
                        grouped[full_head][:, kind].rearrange("p k c t -> p (k c t)"),
                        codes[:, kind].rearrange("p k c -> p (k c)"),
                        scales[:, kind].rearrange("p k c -> p (k c)"),
                    )

            if step < all_heads:
                nc.vector.scalar_tensor_tensor(
                    out=grouped[step][:, KEYS],
                    in0=k_bank,
                    scalar=0.0,
                    in1=exp_k[:],
                    op0=ALU.max,
                    op1=ALU.add,
                )
                if step in X_AHEAD:
                    half = X_AHEAD.index(step)
                    for t in (2 * half, 2 * half + 1):
                        waiting.extend(transpose_x(1, t))

            newest = step - CONTEXT_LAG
            if 0 <= newest < all_heads - GROUP and newest % GROUP == GROUP - 1:
                turn = newest // GROUP % 2 or step >= all_heads
                context(newest + 1 - GROUP, GROUP, nc.scalar.copy if turn else nc.vector.tensor_copy)
        context(all_heads - 2, 1, nc.scalar.copy)
        context(all_heads - 1, 1, nc.vector.tensor_copy)
